import numpy as np
import ml_dtypes


def mxq(x, axis, fmt="e4m3"):
    dtype, down = {"e4m3": (ml_dtypes.float8_e4m3fn, 7), "e5m2": (ml_dtypes.float8_e5m2, 14)}[fmt]
    v = np.moveaxis(np.asarray(x, np.float32).astype(ml_dtypes.bfloat16).astype(np.float64), axis, -1)
    blocks = v.reshape(v.shape[:-1] + (-1, 32))
    amax = np.abs(blocks).max(-1, keepdims=True)
    byte = np.maximum(np.where(amax > 0, np.frexp(amax)[1] - 1 + 127, 0) - down, 1)
    scale = np.exp2(byte - 127.0)
    codes = (blocks / scale).astype(np.float32).astype(dtype).astype(np.float64)
    return np.moveaxis((codes * scale).reshape(v.shape), -1, axis)


WIDE = False


def mx_kscale(k):
    if not WIDE:
        return np.ones(k)
    levels = np.array([10, -10, 5, -5, 0])
    if k % 512:
        return np.exp2(np.random.permutation(np.resize(levels, k // 32))).repeat(32)
    a = np.empty((k // 512, 16))
    for p in range(k // 512):
        a[p, :8] = np.random.permutation(np.resize(levels, 8))
        for g in range(8):
            far = levels[np.abs(levels - a[p, g]) >= 10]
            a[p, g + 8] = far[np.random.randint(len(far))]
    return np.exp2(a.ravel()).repeat(32)


BF16 = ml_dtypes.bfloat16


def bf(x):
    return np.asarray(x, np.float32).astype(BF16)


def f64(x):
    return np.asarray(x).astype(np.float64)


B, T, KA, KT, DIM, NH, HD, E = 16, 512, 256, 256, 512, 8, 128, 8
EPS = 1e-5


def draw0():
    r = np.random.standard_normal
    s = mx_kscale(DIM)
    t = mx_kscale(DIM)
    return {"h_attn": bf(r((B, T, DIM)) * 0.4 * s),
            "x": bf(r((B, T, DIM))),
            "W_o": bf(r((DIM, DIM)) * 2.0 / np.sqrt(DIM) / s[None, :]),
            "b_o": bf(r(DIM) * 0.3 + 0.2),
            "W_ffn": bf(r((DIM, DIM)) / np.sqrt(DIM) / t[None, :]),
            "b_ffn": bf(r(DIM) * 0.3),
            "gamma": bf((1.0 + 0.1 * r(DIM)) * t),
            "beta": bf(0.2 * r(DIM) * t)}


def core(h_attn, x, W_o, b_o, W_ffn, b_ffn, gamma, beta):
    y = (mxq(f64(h_attn), 2, "e4m3") @ mxq(f64(W_o), 1, "e4m3").T) + f64(b_o) + f64(x)
    mu = y.mean(-1, keepdims=True)
    var = ((y - mu) ** 2).mean(-1, keepdims=True)
    xn = (y - mu) / np.sqrt(var + EPS) * f64(gamma) + f64(beta)
    return np.maximum((mxq(xn, 2, "e4m3") @ mxq(f64(W_ffn), 1, "e4m3").T) + f64(b_ffn), 0.0)


def e4m3fn_bytes(y):
    return np.clip(np.asarray(y, np.float64), -448.0, 448.0).astype(np.float32).astype(ml_dtypes.float8_e4m3fn).view(np.uint8)


def e4m3fn_values(b):
    return np.asarray(b, np.uint8).view(ml_dtypes.float8_e4m3fn).astype(np.float64)


def setup_inputs():
    d = draw0()
    x0 = np.asarray(d['h_attn']).astype(np.float64)
    s = (np.max(np.abs(x0), axis=(0, 1), keepdims=True) / 448.0).astype(np.float32)
    out = {}
    for k, v in d.items():
        if k == 'h_attn':
            out['h_attn_bytes'] = e4m3fn_bytes(x0 / s.astype(np.float64))
            out['h_attn_scale'] = s
        else:
            out[k] = v
    return out


def reference(h_attn_bytes, h_attn_scale, x, W_o, b_o, W_ffn, b_ffn, gamma, beta):
    return core(e4m3fn_values(h_attn_bytes) * h_attn_scale.astype(np.float64), x, W_o, b_o, W_ffn, b_ffn, gamma, beta)

@@ -1,0 +1,290 @@
+from contextlib import ExitStack
+
+import concourse.mybir as mybir
+from concourse.masks import make_identity
+
+F32 = mybir.dt.float32
+BF16 = mybir.dt.bfloat16
+U32 = mybir.dt.uint32
+U8 = mybir.dt.uint8
+FP8 = mybir.dt.float8_e4m3fn
+FP8X4 = mybir.dt.float8_e4m3fn_x4
+ACT = mybir.ActivationFunctionType
+ALU = mybir.AluOpType
+
+P = 128
+D = 512
+TOKENS = 16 * 512
+J = 2
+STEPS = TOKENS // (P * J)
+EPS = 1e-5
+FLOPS = 2 * 2 * TOKENS * D * D
+
+
+def tile_l1regressionmoeactionhead_pc_t_kernel(
+    tc, h_bytes, h_scale, x, w_o, b_o, w_ffn, b_ffn, gamma, beta, out
+):
+    nc = tc.nc
+    hb_view = h_bytes.rearrange("b t d -> (b t) d").rearrange("(s p j) d -> s p j d", p=P, j=J)
+    x_view = x.rearrange("b t d -> (b t) d").rearrange("(s p j) d -> s p j d", p=P, j=J)
+    out_view = out.rearrange("b t d -> (b t) d").rearrange("(s p j) d -> s p j d", p=P, j=J)
+
+    with ExitStack() as ctx:
+        keep = ctx.enter_context(tc.tile_pool(name="keep", bufs=1))
+        pool = ctx.enter_context(tc.tile_pool(name="work", bufs=3))
+        psum = ctx.enter_context(tc.psum_pool(name="psum", bufs=2))
+
+        state = {}
+
+        def load(s):
+            raw8 = pool.tile([P, J * D], U8, name="raw8", bufs=5)
+            nc.sync.dma_start(out=raw8[:].rearrange("p (j d) -> p j d", j=J), in_=hb_view[s])
+            xt = pool.tile([P, J, D], BF16, name="xt", bufs=6)
+            nc.sync.dma_start(out=xt[:], in_=x_view[s])
+            state["raw8", s] = raw8
+            state["xt", s] = xt
+
+        hs = keep.tile([P, J, D], F32, name="hs")
+        nc.sync.dma_start(out=hs[:, 0, :], in_=h_scale.rearrange("a b d -> (a b d)").partition_broadcast(P))
+        wo_raw = keep.tile([P, 4, D], BF16, name="wo_raw")
+        nc.sync.dma_start(out=wo_raw[:], in_=w_o.rearrange("(m t) k -> m t k", t=4))
+        load(0)
+        bo = keep.tile([P, D], BF16, name="bo")
+        nc.sync.dma_start(out=bo[:], in_=b_o.partition_broadcast(P))
+        load(1)
+        g16 = keep.tile([P, 4], BF16, name="g16")
+        nc.sync.dma_start(out=g16[:], in_=gamma.rearrange("(p t) -> p t", t=4))
+        b16 = keep.tile([P, 4], BF16, name="b16")
+        nc.sync.dma_start(out=b16[:], in_=beta.rearrange("(p t) -> p t", t=4))
+        wf_raw = keep.tile([P, 4, D], BF16, name="wf_raw")
+        nc.sync.dma_start(out=wf_raw[:], in_=w_ffn.rearrange("(a m) k -> m a k", a=4))
+        load(2)
+        load(3)
+        bfn = keep.tile([P, D], BF16, name="bfn")
+        nc.sync.dma_start(out=bfn[:], in_=b_ffn.partition_broadcast(P))
+        ident = keep.tile([P, P], F32, name="ident")
+        make_identity(nc, ident[:])
+        nc.vector.tensor_copy(out=hs[:, 1, :], in_=hs[:, 0, :])
+
+        def weight(raw, name):
+            grouped = keep.tile([P, D * 4], BF16, name=name + "_g", align_bytes=64)
+            codes = keep.tile([P, D], U32, name=name + "_c", align_bytes=64)
+            scales = keep.tile([P, D], U8, name=name + "_s", align_bytes=64)
+            words = grouped[:].bitcast(F32).rearrange("p (h s n u) -> p h s n u", h=2, s=2, u=2)
+            for h in range(2):
+                wt = psum.tile([P, 2, 2, P], F32, name="wt", tag="zt")
+                for s in range(2):
+                    src = raw[:, 2 * h + s, :].bitcast(F32)
+                    for u in range(2):
+                        nc.tensor.transpose(wt[:, s, u, :], src[:, u : D // 2 : 2], ident[:])
+                nc.scalar.copy(out=words[:, h], in_=wt[:].rearrange("p s u n -> p s n u"))
+            nc.vector.quantize_mx(out=codes[:].bitcast(FP8X4), scales=scales[:], in_=grouped[:])
+            return codes, scales
+
+        def widen(s):
+            hb = pool.tile([P, J * D], BF16, name="hb")
+            nc.vector.tensor_tensor(
+                out=hb[:],
+                in0=state["raw8", s][:].bitcast(FP8),
+                in1=hs[:].rearrange("p j d -> p (j d)"),
+                op=ALU.mult,
+            )
+            state["hb", s] = hb
+
+        def turn_h(s):
+            ht = psum.tile([P, J, 2, P], F32, name="ht")
+            words = state["hb", s][:].bitcast(F32)
+            for j in range(J):
+                for u in range(2):
+                    nc.tensor.transpose(ht[:, j, u, :], words[:, 256 * j + u : 256 * (j + 1) : 2], ident[:])
+            state["ht", s] = ht
+
+        def copy_h(s):
+            hg = pool.tile([P, J * D], BF16, name="hg", align_bytes=64)
+            nc.scalar.copy(
+                out=hg[:].bitcast(F32).rearrange("p (j n u) -> p j n u", j=J, u=2),
+                in_=state["ht", s][:].rearrange("p j u n -> p j n u"),
+            )
+            state["hg", s] = hg
+
+        def quant(s, src, dst):
+            codes = pool.tile([P, J * P], U32, name=dst + "_c", align_bytes=64)
+            scales = pool.tile([P, J * P], U8, name=dst + "_s", align_bytes=64)
+            nc.vector.quantize_mx(out=codes[:].bitcast(FP8X4), scales=scales[:], in_=state[src, s][:])
+            state[dst, s] = (codes, scales)
+
+        def mx(s, j, operand, weights, tag):
+            codes, scales = state[operand, s]
+            acc = psum.tile([P, D], F32, name=tag)
+            c = slice(P * j, P * (j + 1))
+            nc.tensor.matmul_mx(
+                out=acc[:],
+                lhsT=codes[:, c].bitcast(FP8X4),
+                lhsT_scale=scales[:, c],
+                rhs=weights[0][:].bitcast(FP8X4),
+                rhs_scale=weights[1][:],
+                start=True,
+                stop=True,
+            )
+            state[tag, s, j] = acc
+
+        def add_xb(s):
+            xb = pool.tile([P, J, 4, P], F32, name="xb")
+            for j in range(J):
+                nc.gpsimd.tensor_tensor(
+                    out=xb[:, j],
+                    in0=state["xt", s][:, j, :].rearrange("p (m t) -> p t m", t=4),
+                    in1=bo[:].rearrange("p (m t) -> p t m", t=4),
+                    op=ALU.add,
+                )
+            state["xb", s] = xb
+
+        def residual(s):
+            y = pool.tile([P, J, D], F32, name="y")
+            total = pool.tile([P, J], F32, name="total")
+            for j in range(J):
+                nc.vector.scalar_tensor_tensor(
+                    out=y[:, j, :],
+                    in0=state["yp", s, j][:],
+                    scalar=1.0,
+                    in1=state["xb", s][:, j].rearrange("p t m -> p (t m)"),
+                    op0=ALU.mult,
+                    op1=ALU.add,
+                    accum_out=total[:, j : j + 1],
+                )
+            state["y", s] = y
+            state["total", s] = total
+
+        def neg_mean(s):
+            nmu = pool.tile([P, J], F32, name="nmu")
+            nc.scalar.activation(out=nmu[:], in_=state["total", s][:], func=ACT.Copy, scale=-1.0 / D)
+            state["nmu", s] = nmu
+
+        def squares(s):
+            ssq = pool.tile([P, J], F32, name="ssq")
+            for j in range(J):
+                junk = pool.tile([P, D], BF16, name="junk")
+                nc.scalar.activation(
+                    out=junk[:],
+                    in_=state["y", s][:, j, :],
+                    func=ACT.Square,
+                    bias=state["nmu", s][:, j : j + 1],
+                    accum_out=ssq[:, j : j + 1],
+                )
+            rstd = pool.tile([P, J], F32, name="rstd")
+            nc.scalar.activation(out=rstd[:], in_=ssq[:], func=ACT.Abs_reciprocal_sqrt, scale=1.0 / D, bias=eps[:])
+            state["rstd", s] = rstd
+            state["z", s] = pool.tile([P, J, D], F32, name="z")
+
+        def norm_v(s):
+            nc.vector.tensor_scalar(
+                out=state["z", s][:, 0, :],
+                in0=state["y", s][:, 0, :],
+                scalar1=state["nmu", s][:, 0:1],
+                scalar2=state["rstd", s][:, 0:1],
+                op0=ALU.add,
+                op1=ALU.mult,
+            )
+
+        def norm_s(s):
+            nmr = pool.tile([P, 1], F32, name="nmr")
+            rstd = state["rstd", s][:, 1:2]
+            nc.scalar.activation(out=nmr[:], in_=state["nmu", s][:, 1:2], func=ACT.Copy, scale=rstd)
+            nc.scalar.activation(
+                out=state["z", s][:, 1, :], in_=state["y", s][:, 1, :], func=ACT.Identity, scale=rstd, bias=nmr[:]
+            )
+
+        def turn_z(s):
+            for b in range(2):
+                zt = psum.tile([P, 2, J * P], F32, name="zt")
+                for i in range(2):
+                    t = 2 * b + i
+                    for j in range(J):
+                        nc.tensor.transpose(
+                            zt[:, i, P * j : P * (j + 1)],
+                            state["z", s][:, j, P * t : P * (t + 1)],
+                            ident[:],
+                        )
+                state["zt", s, b] = zt
+
+        def affine(s):
+            xp = pool.tile([P, 4, J * P], BF16, name="xp")
+            for t in range(4):
+                nc.scalar.activation(
+                    out=xp[:, t, :],
+                    in_=state["zt", s, t // 2][:, t % 2, :],
+                    func=ACT.Identity,
+                    scale=gam[:, 0, t : t + 1],
+                    bias=gam[:, 1, t : t + 1],
+                )
+            state["xp", s] = xp
+
+        def interleave(s):
+            xg = pool.tile([P, J * D], BF16, name="xg", align_bytes=64)
+            nc.vector.tensor_copy(
+                out=xg[:].rearrange("p (c i t) -> p c t i", i=4, t=4),
+                in_=state["xp", s][:].rearrange("p t (c i) -> p c t i", i=4),
+            )
+            state["xg", s] = xg
+
+        def bias_out(s):
+            ot = pool.tile([P, J, D], F32, name="ot")
+            for j in range(J):
+                nc.vector.tensor_tensor(out=ot[:, j, :], in0=state["op", s, j][:], in1=bfn[:], op=ALU.add)
+            state["ot", s] = ot
+
+        def relu(s):
+            ot = state["ot", s]
+            for j in range(J):
+                nc.scalar.activation(out=ot[:, j, :], in_=ot[:, j, :], func=ACT.Relu)
+            nc.sync.dma_start(out=out_view[s], in_=ot[:])
+
+        eps = keep.tile([P, 1], F32, name="eps")
+        nc.gpsimd.memset(eps[:], EPS)
+        gam = keep.tile([P, 2, 4], F32, name="gam")
+
+        wo = weight(wo_raw, "wo")
+        wf = None
+
+        def live(s):
+            return 0 <= s < STEPS
+
+        for s in range(-2, STEPS + 2):
+            if s >= 0 and live(s + 4):
+                load(s + 4)
+            if live(s + 1):
+                add_xb(s + 1)
+            if live(s + 1):
+                copy_h(s + 1)
+            if live(s - 1):
+                affine(s - 1)
+            if live(s):
+                residual(s)
+                neg_mean(s)
+                squares(s)
+            if live(s + 2):
+                widen(s + 2)
+                turn_h(s + 2)
+            if live(s - 1):
+                interleave(s - 1)
+            if live(s):
+                norm_v(s)
+                norm_s(s)
+            if live(s - 1):
+                quant(s - 1, "xg", "xq")
+                for j in range(J):
+                    mx(s - 1, j, "xq", wf, "op")
+            if live(s + 1):
+                quant(s + 1, "hg", "hq")
+                for j in range(J):
+                    mx(s + 1, j, "hq", wo, "yp")
+            if live(s):
+                turn_z(s)
+            if s == -1:
+                wf = weight(wf_raw, "wf")
+                nc.vector.tensor_copy(out=gam[:, 0, :], in_=g16[:])
+                nc.vector.tensor_copy(out=gam[:, 1, :], in_=b16[:])
+            if live(s - 2):
+                relu(s - 2)
+            if live(s - 1):
+                bias_out(s - 1)

@@ -31,15 +31,16 @@ def tile_l1regressionmoeactionhead_pc_t_kernel(
 
     with ExitStack() as ctx:
         keep = ctx.enter_context(tc.tile_pool(name="keep", bufs=1))
-        pool = ctx.enter_context(tc.tile_pool(name="work", bufs=3))
+        pool = ctx.enter_context(tc.tile_pool(name="work", bufs=4))
         psum = ctx.enter_context(tc.psum_pool(name="psum", bufs=2))
+        ctx.enter_context(tc.manual_schedule())
 
         state = {}
 
         def load(s):
-            raw8 = pool.tile([P, J * D], U8, name="raw8", bufs=5)
+            raw8 = pool.tile([P, J * D], U8, name="raw8", bufs=6)
             nc.sync.dma_start(out=raw8[:].rearrange("p (j d) -> p j d", j=J), in_=hb_view[s])
-            xt = pool.tile([P, J, D], BF16, name="xt", bufs=6)
+            xt = pool.tile([P, J, D], BF16, name="xt", bufs=8)
             nc.sync.dma_start(out=xt[:], in_=x_view[s])
             state["raw8", s] = raw8
             state["xt", s] = xt
@@ -49,9 +50,9 @@ def tile_l1regressionmoeactionhead_pc_t_kernel(
         wo_raw = keep.tile([P, 4, D], BF16, name="wo_raw")
         nc.sync.dma_start(out=wo_raw[:], in_=w_o.rearrange("(m t) k -> m t k", t=4))
         load(0)
+        load(1)
         bo = keep.tile([P, D], BF16, name="bo")
         nc.sync.dma_start(out=bo[:], in_=b_o.partition_broadcast(P))
-        load(1)
         g16 = keep.tile([P, 4], BF16, name="g16")
         nc.sync.dma_start(out=g16[:], in_=gamma.rearrange("(p t) -> p t", t=4))
         b16 = keep.tile([P, 4], BF16, name="b16")
@@ -60,6 +61,7 @@ def tile_l1regressionmoeactionhead_pc_t_kernel(
         nc.sync.dma_start(out=wf_raw[:], in_=w_ffn.rearrange("(a m) k -> m a k", a=4))
         load(2)
         load(3)
+        load(4)
         bfn = keep.tile([P, D], BF16, name="bfn")
         nc.sync.dma_start(out=bfn[:], in_=b_ffn.partition_broadcast(P))
         ident = keep.tile([P, P], F32, name="ident")
@@ -128,96 +130,105 @@ def tile_l1regressionmoeactionhead_pc_t_kernel(
             )
             state[tag, s, j] = acc
 
-        def add_xb(s):
-            xb = pool.tile([P, J, 4, P], F32, name="xb")
-            for j in range(J):
-                nc.gpsimd.tensor_tensor(
-                    out=xb[:, j],
-                    in0=state["xt", s][:, j, :].rearrange("p (m t) -> p t m", t=4),
-                    in1=bo[:].rearrange("p (m t) -> p t m", t=4),
-                    op=ALU.add,
-                )
-            state["xb", s] = xb
+        def gate(s):
+            nc.vector.tensor_copy(out=bo_live[:, 0:2], in_=bo[:, 0:2])
+            state["xb", s] = pool.tile([P, J, 4, P], F32, name="xb")
 
-        def residual(s):
-            y = pool.tile([P, J, D], F32, name="y")
-            total = pool.tile([P, J], F32, name="total")
-            for j in range(J):
-                nc.vector.scalar_tensor_tensor(
-                    out=y[:, j, :],
-                    in0=state["yp", s, j][:],
-                    scalar=1.0,
-                    in1=state["xb", s][:, j].rearrange("p t m -> p (t m)"),
-                    op0=ALU.mult,
-                    op1=ALU.add,
-                    accum_out=total[:, j : j + 1],
-                )
-            state["y", s] = y
-            state["total", s] = total
+        def add_xb(s, j):
+            nc.gpsimd.tensor_tensor(
+                out=state["xb", s][:, j],
+                in0=state["xt", s][:, j, :].rearrange("p (m t) -> p t m", t=4),
+                in1=bo_live[:].rearrange("p (m t) -> p t m", t=4),
+                op=ALU.add,
+            )
+
+        def residual(s, j):
+            if j == 0:
+                state["y", s] = pool.tile([P, J, D], F32, name="y")
+                state["total", s] = pool.tile([P, J], F32, name="total")
+            nc.vector.scalar_tensor_tensor(
+                out=state["y", s][:, j, :],
+                in0=state["yp", s, j][:],
+                scalar=1.0,
+                in1=state["xb", s][:, j].rearrange("p t m -> p (t m)"),
+                op0=ALU.mult,
+                op1=ALU.add,
+                accum_out=state["total", s][:, j : j + 1],
+            )
 
         def neg_mean(s):
             nmu = pool.tile([P, J], F32, name="nmu")
             nc.scalar.activation(out=nmu[:], in_=state["total", s][:], func=ACT.Copy, scale=-1.0 / D)
             state["nmu", s] = nmu
+            state["ssq", s] = pool.tile([P, J], F32, name="ssq")
 
-        def squares(s):
-            ssq = pool.tile([P, J], F32, name="ssq")
-            for j in range(J):
-                junk = pool.tile([P, D], BF16, name="junk")
-                nc.scalar.activation(
-                    out=junk[:],
-                    in_=state["y", s][:, j, :],
-                    func=ACT.Square,
-                    bias=state["nmu", s][:, j : j + 1],
-                    accum_out=ssq[:, j : j + 1],
-                )
+        def squares(s, j):
+            junk = pool.tile([P, D], BF16, name="junk")
+            nc.scalar.activation(
+                out=junk[:],
+                in_=state["y", s][:, j, :],
+                func=ACT.Square,
+                bias=state["nmu", s][:, j : j + 1],
+                accum_out=state["ssq", s][:, j : j + 1],
+            )
+
+        def rstd_of(s):
             rstd = pool.tile([P, J], F32, name="rstd")
-            nc.scalar.activation(out=rstd[:], in_=ssq[:], func=ACT.Abs_reciprocal_sqrt, scale=1.0 / D, bias=eps[:])
+            nc.scalar.activation(
+                out=rstd[:], in_=state["ssq", s][:], func=ACT.Abs_reciprocal_sqrt, scale=1.0 / D, bias=eps[:]
+            )
             state["rstd", s] = rstd
             state["z", s] = pool.tile([P, J, D], F32, name="z")
 
-        def norm_v(s):
+        def norm_v(s, j):
             nc.vector.tensor_scalar(
-                out=state["z", s][:, 0, :],
-                in0=state["y", s][:, 0, :],
-                scalar1=state["nmu", s][:, 0:1],
-                scalar2=state["rstd", s][:, 0:1],
+                out=state["z", s][:, j, :],
+                in0=state["y", s][:, j, :],
+                scalar1=state["nmu", s][:, j : j + 1],
+                scalar2=state["rstd", s][:, j : j + 1],
                 op0=ALU.add,
                 op1=ALU.mult,
             )
 
-        def norm_s(s):
+        def neg_mean_rstd(s, j):
             nmr = pool.tile([P, 1], F32, name="nmr")
-            rstd = state["rstd", s][:, 1:2]
-            nc.scalar.activation(out=nmr[:], in_=state["nmu", s][:, 1:2], func=ACT.Copy, scale=rstd)
             nc.scalar.activation(
-                out=state["z", s][:, 1, :], in_=state["y", s][:, 1, :], func=ACT.Identity, scale=rstd, bias=nmr[:]
+                out=nmr[:], in_=state["nmu", s][:, j : j + 1], func=ACT.Copy, scale=state["rstd", s][:, j : j + 1]
+            )
+            state["nmr", s, j] = nmr
+
+        def norm_s(s, j):
+            nc.scalar.activation(
+                out=state["z", s][:, j, :],
+                in_=state["y", s][:, j, :],
+                func=ACT.Identity,
+                scale=state["rstd", s][:, j : j + 1],
+                bias=state["nmr", s, j][:],
             )
 
-        def turn_z(s):
-            for b in range(2):
-                zt = psum.tile([P, 2, J * P], F32, name="zt")
-                for i in range(2):
-                    t = 2 * b + i
-                    for j in range(J):
-                        nc.tensor.transpose(
-                            zt[:, i, P * j : P * (j + 1)],
-                            state["z", s][:, j, P * t : P * (t + 1)],
-                            ident[:],
-                        )
-                state["zt", s, b] = zt
+        def turn_z(s, b):
+            zt = psum.tile([P, 2, J * P], F32, name="zt")
+            for i in range(2):
+                t = 2 * b + i
+                for j in range(J):
+                    nc.tensor.transpose(
+                        zt[:, i, P * j : P * (j + 1)],
+                        state["z", s][:, j, P * t : P * (t + 1)],
+                        ident[:],
+                    )
+            state["zt", s, b] = zt
 
-        def affine(s):
-            xp = pool.tile([P, 4, J * P], BF16, name="xp")
-            for t in range(4):
+        def affine(s, b):
+            if b == 0:
+                state["xp", s] = pool.tile([P, 4, J * P], BF16, name="xp")
+            for t in (2 * b, 2 * b + 1):
                 nc.scalar.activation(
-                    out=xp[:, t, :],
-                    in_=state["zt", s, t // 2][:, t % 2, :],
+                    out=state["xp", s][:, t, :],
+                    in_=state["zt", s, b][:, t % 2, :],
                     func=ACT.Identity,
                     scale=gam[:, 0, t : t + 1],
                     bias=gam[:, 1, t : t + 1],
                 )
-            state["xp", s] = xp
 
         def interleave(s):
             xg = pool.tile([P, J * D], BF16, name="xg", align_bytes=64)
@@ -227,64 +238,68 @@ def tile_l1regressionmoeactionhead_pc_t_kernel(
             )
             state["xg", s] = xg
 
-        def bias_out(s):
-            ot = pool.tile([P, J, D], F32, name="ot")
-            for j in range(J):
-                nc.vector.tensor_tensor(out=ot[:, j, :], in0=state["op", s, j][:], in1=bfn[:], op=ALU.add)
-            state["ot", s] = ot
+        def bias_out(s, j):
+            if j == 0:
+                state["ot", s] = pool.tile([P, J, D], F32, name="ot")
+            nc.vector.tensor_tensor(out=state["ot", s][:, j, :], in0=state["op", s, j][:], in1=bfn[:], op=ALU.add)
 
-        def relu(s):
+        def relu(s, j):
             ot = state["ot", s]
-            for j in range(J):
-                nc.scalar.activation(out=ot[:, j, :], in_=ot[:, j, :], func=ACT.Relu)
-            nc.sync.dma_start(out=out_view[s], in_=ot[:])
+            nc.scalar.activation(out=ot[:, j, :], in_=ot[:, j, :], func=ACT.Relu)
+            if j == J - 1:
+                nc.sync.dma_start(out=out_view[s], in_=ot[:])
 
         eps = keep.tile([P, 1], F32, name="eps")
         nc.gpsimd.memset(eps[:], EPS)
         gam = keep.tile([P, 2, 4], F32, name="gam")
+        bo_live = keep.tile([P, D], BF16, name="bo_live")
 
         wo = weight(wo_raw, "wo")
         wf = None
 
-        def live(s):
-            return 0 <= s < STEPS
-
-        for s in range(-2, STEPS + 2):
-            if s >= 0 and live(s + 4):
-                load(s + 4)
-            if live(s + 1):
-                add_xb(s + 1)
-            if live(s + 1):
-                copy_h(s + 1)
-            if live(s - 1):
-                affine(s - 1)
-            if live(s):
-                residual(s)
-                neg_mean(s)
-                squares(s)
-            if live(s + 2):
-                widen(s + 2)
-                turn_h(s + 2)
-            if live(s - 1):
-                interleave(s - 1)
-            if live(s):
-                norm_v(s)
-                norm_s(s)
-            if live(s - 1):
-                quant(s - 1, "xg", "xq")
-                for j in range(J):
-                    mx(s - 1, j, "xq", wf, "op")
-            if live(s + 1):
-                quant(s + 1, "hg", "hq")
-                for j in range(J):
-                    mx(s + 1, j, "hq", wo, "yp")
-            if live(s):
-                turn_z(s)
-            if s == -1:
+        order = [
+            (lambda s: residual(s, 0), 0),
+            (lambda s: affine(s, 1), -3),
+            (lambda s: add_xb(s, 0), 1),
+            (lambda s: residual(s, 1), 0),
+            (copy_h, 2),
+            (lambda s: neg_mean_rstd(s, 1), -1),
+            (lambda s: bias_out(s, 0), -6),
+            (lambda s: relu(s, 0), -7),
+            (lambda s: add_xb(s, 1), 1),
+            (lambda s: bias_out(s, 1), -6),
+            (neg_mean, 0),
+            (lambda s: relu(s, 1), -7),
+            (lambda s: mx(s, 0, "xq", wf, "op"), -5),
+            (lambda s: quant(s, "xg", "xq"), -4),
+            (lambda s: squares(s, 1), 0),
+            (lambda s: mx(s, 1, "xq", wf, "op"), -5),
+            (lambda s: quant(s, "hg", "hq"), 1),
+            (lambda s: norm_v(s, 0), -2),
+            (lambda s: squares(s, 0), 0),
+            (lambda s: mx(s, 0, "hq", wo, "yp"), 1),
+            (widen, 3),
+            (lambda s: turn_z(s, 0), -2),
+            (lambda s: norm_s(s, 1), -1),
+            (lambda s: mx(s, 1, "hq", wo, "yp"), 1),
+            (lambda s: turn_z(s, 1), -2),
+            (lambda s: affine(s, 0), -2),
+            (interleave, -3),
+            (turn_h, 3),
+            (rstd_of, 0),
+            (gate, 2),
+        ]
+        first = -max(offset for stage, offset in order)
+        last = STEPS - min(offset for stage, offset in order)
+        for r in range(first, last):
+            if r == -1:
                 wf = weight(wf_raw, "wf")
                 nc.vector.tensor_copy(out=gam[:, 0, :], in_=g16[:])
                 nc.vector.tensor_copy(out=gam[:, 1, :], in_=b16[:])
-            if live(s - 2):
-                relu(s - 2)
-            if live(s - 1):
-                bias_out(s - 1)
+            if r == first + 1:
+                nc.vector.tensor_copy(out=bo_live[:], in_=bo[:])
+            if 5 <= r + 6 < STEPS:
+                load(r + 6)
+            for stage, offset in order:
+                if 0 <= r + offset < STEPS:
+                    stage(r + offset)

@@ -18,6 +18,7 @@ TOKENS = 16 * 512
 J = 2
 STEPS = TOKENS // (P * J)
 EPS = 1e-5
+XG = 400
 FLOPS = 2 * 2 * TOKENS * D * D
 
 
@@ -37,33 +38,40 @@ def tile_l1regressionmoeactionhead_pc_t_kernel(
 
         state = {}
 
-        def load(s):
+        def load_h(s):
             raw8 = pool.tile([P, J * D], U8, name="raw8", bufs=6)
             nc.sync.dma_start(out=raw8[:].rearrange("p (j d) -> p j d", j=J), in_=hb_view[s])
+            state["raw8", s] = raw8
+
+        def load_x(s):
             xt = pool.tile([P, J, D], BF16, name="xt", bufs=8)
             nc.sync.dma_start(out=xt[:], in_=x_view[s])
-            state["raw8", s] = raw8
             state["xt", s] = xt
 
+        load_h(0)
         hs = keep.tile([P, J, D], F32, name="hs")
         nc.sync.dma_start(out=hs[:, 0, :], in_=h_scale.rearrange("a b d -> (a b d)").partition_broadcast(P))
         wo_raw = keep.tile([P, 4, D], BF16, name="wo_raw")
-        nc.sync.dma_start(out=wo_raw[:], in_=w_o.rearrange("(m t) k -> m t k", t=4))
-        load(0)
-        load(1)
+        nc.sync.dma_start(out=wo_raw[:], in_=w_o.rearrange("(a m) k -> m a k", a=4))
+        load_h(1)
         bo = keep.tile([P, D], BF16, name="bo")
         nc.sync.dma_start(out=bo[:], in_=b_o.partition_broadcast(P))
+        load_x(0)
+        load_h(2)
+        load_x(1)
         g16 = keep.tile([P, 4], BF16, name="g16")
         nc.sync.dma_start(out=g16[:], in_=gamma.rearrange("(p t) -> p t", t=4))
         b16 = keep.tile([P, 4], BF16, name="b16")
         nc.sync.dma_start(out=b16[:], in_=beta.rearrange("(p t) -> p t", t=4))
         wf_raw = keep.tile([P, 4, D], BF16, name="wf_raw")
         nc.sync.dma_start(out=wf_raw[:], in_=w_ffn.rearrange("(a m) k -> m a k", a=4))
-        load(2)
-        load(3)
-        load(4)
+        load_h(3)
+        load_x(2)
         bfn = keep.tile([P, D], BF16, name="bfn")
         nc.sync.dma_start(out=bfn[:], in_=b_ffn.partition_broadcast(P))
+        load_h(4)
+        load_x(3)
+        load_x(4)
         ident = keep.tile([P, P], F32, name="ident")
         make_identity(nc, ident[:])
         nc.vector.tensor_copy(out=hs[:, 1, :], in_=hs[:, 0, :])
@@ -131,15 +139,19 @@ def tile_l1regressionmoeactionhead_pc_t_kernel(
             state[tag, s, j] = acc
 
         def gate(s):
-            nc.vector.tensor_copy(out=bo_live[:, 0:2], in_=bo[:, 0:2])
-            state["xb", s] = pool.tile([P, J, 4, P], F32, name="xb")
+            nc.vector.tensor_copy(out=bo_live[:, 0, 0:2], in_=bo2[:, 0, 0:2])
 
-        def add_xb(s, j):
+        def add_xb(s):
+            c = slice(0, XG)
             nc.gpsimd.tensor_tensor(
-                out=state["xb", s][:, j],
-                in0=state["xt", s][:, j, :].rearrange("p (m t) -> p t m", t=4),
-                in1=bo_live[:].rearrange("p (m t) -> p t m", t=4),
-                op=ALU.add,
+                out=state["xb", s][:, :, c], in0=state["xt", s][:, :, c], in1=bo_live[:, :, c], op=ALU.add
+            )
+
+        def add_xb_v(s):
+            state["xb", s] = pool.tile([P, J, D], F32, name="xb")
+            c = slice(XG, D)
+            nc.vector.tensor_tensor(
+                out=state["xb", s][:, :, c], in0=state["xt", s][:, :, c], in1=bo2[:, :, c], op=ALU.add
             )
 
         def residual(s, j):
@@ -150,7 +162,7 @@ def tile_l1regressionmoeactionhead_pc_t_kernel(
                 out=state["y", s][:, j, :],
                 in0=state["yp", s, j][:],
                 scalar=1.0,
-                in1=state["xb", s][:, j].rearrange("p t m -> p (t m)"),
+                in1=state["xb", s][:, j, :],
                 op0=ALU.mult,
                 op1=ALU.add,
                 accum_out=state["total", s][:, j : j + 1],
@@ -180,16 +192,6 @@ def tile_l1regressionmoeactionhead_pc_t_kernel(
             state["rstd", s] = rstd
             state["z", s] = pool.tile([P, J, D], F32, name="z")
 
-        def norm_v(s, j):
-            nc.vector.tensor_scalar(
-                out=state["z", s][:, j, :],
-                in0=state["y", s][:, j, :],
-                scalar1=state["nmu", s][:, j : j + 1],
-                scalar2=state["rstd", s][:, j : j + 1],
-                op0=ALU.add,
-                op1=ALU.mult,
-            )
-
         def neg_mean_rstd(s, j):
             nmr = pool.tile([P, 1], F32, name="nmr")
             nc.scalar.activation(
@@ -213,22 +215,31 @@ def tile_l1regressionmoeactionhead_pc_t_kernel(
                 for j in range(J):
                     nc.tensor.transpose(
                         zt[:, i, P * j : P * (j + 1)],
-                        state["z", s][:, j, P * t : P * (t + 1)],
+                        state["z", s][:, j, t:D:4],
                         ident[:],
                     )
             state["zt", s, b] = zt
 
-        def affine(s, b):
-            if b == 0:
+        def affine(s, t):
+            if t == 0:
                 state["xp", s] = pool.tile([P, 4, J * P], BF16, name="xp")
-            for t in (2 * b, 2 * b + 1):
-                nc.scalar.activation(
-                    out=state["xp", s][:, t, :],
-                    in_=state["zt", s, b][:, t % 2, :],
-                    func=ACT.Identity,
-                    scale=gam[:, 0, t : t + 1],
-                    bias=gam[:, 1, t : t + 1],
-                )
+            nc.scalar.activation(
+                out=state["xp", s][:, t, :],
+                in_=state["zt", s, t // 2][:, t % 2, :],
+                func=ACT.Identity,
+                scale=gam[:, 0, t : t + 1],
+                bias=gam[:, 1, t : t + 1],
+            )
+
+        def affine_v(s, t):
+            nc.vector.tensor_scalar(
+                out=state["xp", s][:, t, :],
+                in0=state["zt", s, t // 2][:, t % 2, :],
+                scalar1=gam[:, 0, t : t + 1],
+                scalar2=gam[:, 1, t : t + 1],
+                op0=ALU.mult,
+                op1=ALU.add,
+            )
 
         def interleave(s):
             xg = pool.tile([P, J * D], BF16, name="xg", align_bytes=64)
@@ -252,54 +263,63 @@ def tile_l1regressionmoeactionhead_pc_t_kernel(
         eps = keep.tile([P, 1], F32, name="eps")
         nc.gpsimd.memset(eps[:], EPS)
         gam = keep.tile([P, 2, 4], F32, name="gam")
-        bo_live = keep.tile([P, D], BF16, name="bo_live")
+        bo_live = keep.tile([P, J, D], BF16, name="bo_live")
+        bo2 = keep.tile([P, J, D], BF16, name="bo2")
 
-        wo = weight(wo_raw, "wo")
+        wo = None
         wf = None
 
         order = [
             (lambda s: residual(s, 0), 0),
-            (lambda s: affine(s, 1), -3),
-            (lambda s: add_xb(s, 0), 1),
+            (lambda s: norm_s(s, 1), -2),
+            (add_xb, 1),
             (lambda s: residual(s, 1), 0),
-            (copy_h, 2),
-            (lambda s: neg_mean_rstd(s, 1), -1),
+            (turn_h, 2),
+            (lambda s: affine(s, 0), -3),
+            (lambda s: affine(s, 1), -3),
             (lambda s: bias_out(s, 0), -6),
-            (lambda s: relu(s, 0), -7),
-            (lambda s: add_xb(s, 1), 1),
+            (rstd_of, -1),
+            (lambda s: affine(s, 2), -3),
+            (copy_h, 2),
             (lambda s: bias_out(s, 1), -6),
+            (lambda s: mx(s, 0, "xq", wf, "op"), -5),
+            (lambda s: neg_mean_rstd(s, 0), -1),
+            (lambda s: neg_mean_rstd(s, 1), -1),
+            (lambda s: affine_v(s, 3), -3),
+            (lambda s: relu(s, 0), -7),
+            (lambda s: mx(s, 1, "xq", wf, "op"), -5),
+            (lambda s: quant(s, "xg", "xq"), -4),
+            (lambda s: quant(s, "hg", "hq"), 1),
             (neg_mean, 0),
             (lambda s: relu(s, 1), -7),
-            (lambda s: mx(s, 0, "xq", wf, "op"), -5),
-            (lambda s: quant(s, "xg", "xq"), -4),
-            (lambda s: squares(s, 1), 0),
-            (lambda s: mx(s, 1, "xq", wf, "op"), -5),
-            (lambda s: quant(s, "hg", "hq"), 1),
-            (lambda s: norm_v(s, 0), -2),
-            (lambda s: squares(s, 0), 0),
-            (lambda s: mx(s, 0, "hq", wo, "yp"), 1),
             (widen, 3),
+            (lambda s: mx(s, 0, "hq", wo, "yp"), 1),
+            (lambda s: squares(s, 1), 0),
             (lambda s: turn_z(s, 0), -2),
-            (lambda s: norm_s(s, 1), -1),
-            (lambda s: mx(s, 1, "hq", wo, "yp"), 1),
-            (lambda s: turn_z(s, 1), -2),
-            (lambda s: affine(s, 0), -2),
+            (lambda s: squares(s, 0), 0),
             (interleave, -3),
-            (turn_h, 3),
-            (rstd_of, 0),
+            (lambda s: mx(s, 1, "hq", wo, "yp"), 1),
+            (lambda s: norm_s(s, 0), -1),
+            (add_xb_v, 2),
+            (lambda s: turn_z(s, 1), -2),
             (gate, 2),
         ]
         first = -max(offset for stage, offset in order)
         last = STEPS - min(offset for stage, offset in order)
         for r in range(first, last):
-            if r == -1:
+            if r == -2:
+                wo = weight(wo_raw, "wo")
+            if r == 1:
                 wf = weight(wf_raw, "wf")
                 nc.vector.tensor_copy(out=gam[:, 0, :], in_=g16[:])
                 nc.vector.tensor_copy(out=gam[:, 1, :], in_=b16[:])
             if r == first + 1:
-                nc.vector.tensor_copy(out=bo_live[:], in_=bo[:])
+                for j in range(J):
+                    nc.vector.tensor_copy(out=bo_live[:, j, :], in_=bo[:])
+                    nc.vector.tensor_copy(out=bo2[:, j, :], in_=bo[:])
             if 5 <= r + 6 < STEPS:
-                load(r + 6)
+                load_h(r + 6)
+                load_x(r + 6)
             for stage, offset in order:
                 if 0 <= r + offset < STEPS:
                     stage(r + offset)

from contextlib import ExitStack

import concourse.mybir as mybir
from concourse.masks import make_identity

F32 = mybir.dt.float32
BF16 = mybir.dt.bfloat16
U32 = mybir.dt.uint32
U8 = mybir.dt.uint8
FP8 = mybir.dt.float8_e4m3fn
FP8X4 = mybir.dt.float8_e4m3fn_x4
ACT = mybir.ActivationFunctionType
ALU = mybir.AluOpType

P = 128
D = 512
TOKENS = 16 * 512
J = 2
STEPS = TOKENS // (P * J)
EPS = 1e-5
XG = 400
FLOPS = 2 * 2 * TOKENS * D * D


def tile_l1regressionmoeactionhead_pc_t_kernel(
    tc, h_bytes, h_scale, x, w_o, b_o, w_ffn, b_ffn, gamma, beta, out
):
    nc = tc.nc
    hb_view = h_bytes.rearrange("b t d -> (b t) d").rearrange("(s p j) d -> s p j d", p=P, j=J)
    x_view = x.rearrange("b t d -> (b t) d").rearrange("(s p j) d -> s p j d", p=P, j=J)
    out_view = out.rearrange("b t d -> (b t) d").rearrange("(s p j) d -> s p j d", p=P, j=J)

    with ExitStack() as ctx:
        keep = ctx.enter_context(tc.tile_pool(name="keep", bufs=1))
        pool = ctx.enter_context(tc.tile_pool(name="work", bufs=4))
        psum = ctx.enter_context(tc.psum_pool(name="psum", bufs=2))
        ctx.enter_context(tc.manual_schedule())

        state = {}

        def load_h(s):
            raw8 = pool.tile([P, J * D], U8, name="raw8", bufs=6)
            nc.sync.dma_start(out=raw8[:].rearrange("p (j d) -> p j d", j=J), in_=hb_view[s])
            state["raw8", s] = raw8

        def load_x(s):
            xt = pool.tile([P, J, D], BF16, name="xt", bufs=8)
            nc.sync.dma_start(out=xt[:], in_=x_view[s])
            state["xt", s] = xt

        load_h(0)
        hs = keep.tile([P, J, D], F32, name="hs")
        nc.sync.dma_start(out=hs[:, 0, :], in_=h_scale.rearrange("a b d -> (a b d)").partition_broadcast(P))
        wo_raw = keep.tile([P, 4, D], BF16, name="wo_raw")
        nc.sync.dma_start(out=wo_raw[:], in_=w_o.rearrange("(a m) k -> m a k", a=4))
        load_h(1)
        bo = keep.tile([P, D], BF16, name="bo")
        nc.sync.dma_start(out=bo[:], in_=b_o.partition_broadcast(P))
        load_x(0)
        load_h(2)
        load_x(1)
        g16 = keep.tile([P, 4], BF16, name="g16")
        nc.sync.dma_start(out=g16[:], in_=gamma.rearrange("(p t) -> p t", t=4))
        b16 = keep.tile([P, 4], BF16, name="b16")
        nc.sync.dma_start(out=b16[:], in_=beta.rearrange("(p t) -> p t", t=4))
        wf_raw = keep.tile([P, 4, D], BF16, name="wf_raw")
        nc.sync.dma_start(out=wf_raw[:], in_=w_ffn.rearrange("(a m) k -> m a k", a=4))
        load_h(3)
        load_x(2)
        bfn = keep.tile([P, D], BF16, name="bfn")
        nc.sync.dma_start(out=bfn[:], in_=b_ffn.partition_broadcast(P))
        load_h(4)
        load_x(3)
        load_x(4)
        ident = keep.tile([P, P], F32, name="ident")
        make_identity(nc, ident[:])
        nc.vector.tensor_copy(out=hs[:, 1, :], in_=hs[:, 0, :])

        def weight(raw, name):
            grouped = keep.tile([P, D * 4], BF16, name=name + "_g", align_bytes=64)
            codes = keep.tile([P, D], U32, name=name + "_c", align_bytes=64)
            scales = keep.tile([P, D], U8, name=name + "_s", align_bytes=64)
            words = grouped[:].bitcast(F32).rearrange("p (h s n u) -> p h s n u", h=2, s=2, u=2)
            for h in range(2):
                wt = psum.tile([P, 2, 2, P], F32, name="wt", tag="zt")
                for s in range(2):
                    src = raw[:, 2 * h + s, :].bitcast(F32)
                    for u in range(2):
                        nc.tensor.transpose(wt[:, s, u, :], src[:, u : D // 2 : 2], ident[:])
                nc.scalar.copy(out=words[:, h], in_=wt[:].rearrange("p s u n -> p s n u"))
            nc.vector.quantize_mx(out=codes[:].bitcast(FP8X4), scales=scales[:], in_=grouped[:])
            return codes, scales

        def widen(s):
            hb = pool.tile([P, J * D], BF16, name="hb")
            nc.vector.tensor_tensor(
                out=hb[:],
                in0=state["raw8", s][:].bitcast(FP8),
                in1=hs[:].rearrange("p j d -> p (j d)"),
                op=ALU.mult,
            )
            state["hb", s] = hb

        def turn_h(s):
            ht = psum.tile([P, J, 2, P], F32, name="ht")
            words = state["hb", s][:].bitcast(F32)
            for j in range(J):
                for u in range(2):
                    nc.tensor.transpose(ht[:, j, u, :], words[:, 256 * j + u : 256 * (j + 1) : 2], ident[:])
            state["ht", s] = ht

        def copy_h(s):
            hg = pool.tile([P, J * D], BF16, name="hg", align_bytes=64)
            nc.scalar.copy(
                out=hg[:].bitcast(F32).rearrange("p (j n u) -> p j n u", j=J, u=2),
                in_=state["ht", s][:].rearrange("p j u n -> p j n u"),
            )
            state["hg", s] = hg

        def quant(s, src, dst):
            codes = pool.tile([P, J * P], U32, name=dst + "_c", align_bytes=64)
            scales = pool.tile([P, J * P], U8, name=dst + "_s", align_bytes=64)
            nc.vector.quantize_mx(out=codes[:].bitcast(FP8X4), scales=scales[:], in_=state[src, s][:])
            state[dst, s] = (codes, scales)

        def mx(s, j, operand, weights, tag):
            codes, scales = state[operand, s]
            acc = psum.tile([P, D], F32, name=tag)
            c = slice(P * j, P * (j + 1))
            nc.tensor.matmul_mx(
                out=acc[:],
                lhsT=codes[:, c].bitcast(FP8X4),
                lhsT_scale=scales[:, c],
                rhs=weights[0][:].bitcast(FP8X4),
                rhs_scale=weights[1][:],
                start=True,
                stop=True,
            )
            state[tag, s, j] = acc

        def gate(s):
            nc.vector.tensor_copy(out=bo_live[:, 0, 0:2], in_=bo2[:, 0, 0:2])

        def add_xb(s):
            c = slice(0, XG)
            nc.gpsimd.tensor_tensor(
                out=state["xb", s][:, :, c], in0=state["xt", s][:, :, c], in1=bo_live[:, :, c], op=ALU.add
            )

        def add_xb_v(s):
            state["xb", s] = pool.tile([P, J, D], F32, name="xb")
            c = slice(XG, D)
            nc.vector.tensor_tensor(
                out=state["xb", s][:, :, c], in0=state["xt", s][:, :, c], in1=bo2[:, :, c], op=ALU.add
            )

        def residual(s, j):
            if j == 0:
                state["y", s] = pool.tile([P, J, D], F32, name="y")
                state["total", s] = pool.tile([P, J], F32, name="total")
            nc.vector.scalar_tensor_tensor(
                out=state["y", s][:, j, :],
                in0=state["yp", s, j][:],
                scalar=1.0,
                in1=state["xb", s][:, j, :],
                op0=ALU.mult,
                op1=ALU.add,
                accum_out=state["total", s][:, j : j + 1],
            )

        def neg_mean(s):
            nmu = pool.tile([P, J], F32, name="nmu")
            nc.scalar.activation(out=nmu[:], in_=state["total", s][:], func=ACT.Copy, scale=-1.0 / D)
            state["nmu", s] = nmu
            state["ssq", s] = pool.tile([P, J], F32, name="ssq")

        def squares(s, j):
            junk = pool.tile([P, D], BF16, name="junk")
            nc.scalar.activation(
                out=junk[:],
                in_=state["y", s][:, j, :],
                func=ACT.Square,
                bias=state["nmu", s][:, j : j + 1],
                accum_out=state["ssq", s][:, j : j + 1],
            )

        def rstd_of(s):
            rstd = pool.tile([P, J], F32, name="rstd")
            nc.scalar.activation(
                out=rstd[:], in_=state["ssq", s][:], func=ACT.Abs_reciprocal_sqrt, scale=1.0 / D, bias=eps[:]
            )
            state["rstd", s] = rstd
            state["z", s] = pool.tile([P, J, D], F32, name="z")

        def neg_mean_rstd(s, j):
            nmr = pool.tile([P, 1], F32, name="nmr")
            nc.scalar.activation(
                out=nmr[:], in_=state["nmu", s][:, j : j + 1], func=ACT.Copy, scale=state["rstd", s][:, j : j + 1]
            )
            state["nmr", s, j] = nmr

        def norm_s(s, j):
            nc.scalar.activation(
                out=state["z", s][:, j, :],
                in_=state["y", s][:, j, :],
                func=ACT.Identity,
                scale=state["rstd", s][:, j : j + 1],
                bias=state["nmr", s, j][:],
            )

        def turn_z(s, b):
            zt = psum.tile([P, 2, J * P], F32, name="zt")
            for i in range(2):
                t = 2 * b + i
                for j in range(J):
                    nc.tensor.transpose(
                        zt[:, i, P * j : P * (j + 1)],
                        state["z", s][:, j, t:D:4],
                        ident[:],
                    )
            state["zt", s, b] = zt

        def affine(s, t):
            if t == 0:
                state["xp", s] = pool.tile([P, 4, J * P], BF16, name="xp")
            nc.scalar.activation(
                out=state["xp", s][:, t, :],
                in_=state["zt", s, t // 2][:, t % 2, :],
                func=ACT.Identity,
                scale=gam[:, 0, t : t + 1],
                bias=gam[:, 1, t : t + 1],
            )

        def affine_v(s, t):
            nc.vector.tensor_scalar(
                out=state["xp", s][:, t, :],
                in0=state["zt", s, t // 2][:, t % 2, :],
                scalar1=gam[:, 0, t : t + 1],
                scalar2=gam[:, 1, t : t + 1],
                op0=ALU.mult,
                op1=ALU.add,
            )

        def interleave(s):
            xg = pool.tile([P, J * D], BF16, name="xg", align_bytes=64)
            nc.vector.tensor_copy(
                out=xg[:].rearrange("p (c i t) -> p c t i", i=4, t=4),
                in_=state["xp", s][:].rearrange("p t (c i) -> p c t i", i=4),
            )
            state["xg", s] = xg

        def bias_out(s, j):
            if j == 0:
                state["ot", s] = pool.tile([P, J, D], F32, name="ot")
            nc.vector.tensor_tensor(out=state["ot", s][:, j, :], in0=state["op", s, j][:], in1=bfn[:], op=ALU.add)

        def relu(s, j):
            ot = state["ot", s]
            nc.scalar.activation(out=ot[:, j, :], in_=ot[:, j, :], func=ACT.Relu)
            if j == J - 1:
                nc.sync.dma_start(out=out_view[s], in_=ot[:])

        eps = keep.tile([P, 1], F32, name="eps")
        nc.gpsimd.memset(eps[:], EPS)
        gam = keep.tile([P, 2, 4], F32, name="gam")
        bo_live = keep.tile([P, J, D], BF16, name="bo_live")
        bo2 = keep.tile([P, J, D], BF16, name="bo2")

        wo = None
        wf = None

        order = [
            (lambda s: residual(s, 0), 0),
            (lambda s: norm_s(s, 1), -2),
            (add_xb, 1),
            (lambda s: residual(s, 1), 0),
            (turn_h, 2),
            (lambda s: affine(s, 0), -3),
            (lambda s: affine(s, 1), -3),
            (lambda s: bias_out(s, 0), -6),
            (rstd_of, -1),
            (lambda s: affine(s, 2), -3),
            (copy_h, 2),
            (lambda s: bias_out(s, 1), -6),
            (lambda s: mx(s, 0, "xq", wf, "op"), -5),
            (lambda s: neg_mean_rstd(s, 0), -1),
            (lambda s: neg_mean_rstd(s, 1), -1),
            (lambda s: affine_v(s, 3), -3),
            (lambda s: relu(s, 0), -7),
            (lambda s: mx(s, 1, "xq", wf, "op"), -5),
            (lambda s: quant(s, "xg", "xq"), -4),
            (lambda s: quant(s, "hg", "hq"), 1),
            (neg_mean, 0),
            (lambda s: relu(s, 1), -7),
            (widen, 3),
            (lambda s: mx(s, 0, "hq", wo, "yp"), 1),
            (lambda s: squares(s, 1), 0),
            (lambda s: turn_z(s, 0), -2),
            (lambda s: squares(s, 0), 0),
            (interleave, -3),
            (lambda s: mx(s, 1, "hq", wo, "yp"), 1),
            (lambda s: norm_s(s, 0), -1),
            (add_xb_v, 2),
            (lambda s: turn_z(s, 1), -2),
            (gate, 2),
        ]
        first = -max(offset for stage, offset in order)
        last = STEPS - min(offset for stage, offset in order)
        for r in range(first, last):
            if r == -2:
                wo = weight(wo_raw, "wo")
            if r == 1:
                wf = weight(wf_raw, "wf")
                nc.vector.tensor_copy(out=gam[:, 0, :], in_=g16[:])
                nc.vector.tensor_copy(out=gam[:, 1, :], in_=b16[:])
            if r == first + 1:
                for j in range(J):
                    nc.vector.tensor_copy(out=bo_live[:, j, :], in_=bo[:])
                    nc.vector.tensor_copy(out=bo2[:, j, :], in_=bo[:])
            if 5 <= r + 6 < STEPS:
                load_h(r + 6)
                load_x(r + 6)
            for stage, offset in order:
                if 0 <= r + offset < STEPS:
                    stage(r + offset)
